import numpy as np
import ml_dtypes


def mxq(x, axis, fmt="e4m3"):
    dtype, down = {"e4m3": (ml_dtypes.float8_e4m3fn, 7), "e5m2": (ml_dtypes.float8_e5m2, 14)}[fmt]
    v = np.moveaxis(np.asarray(x, np.float32).astype(ml_dtypes.bfloat16).astype(np.float64), axis, -1)
    blocks = v.reshape(v.shape[:-1] + (-1, 32))
    amax = np.abs(blocks).max(-1, keepdims=True)
    byte = np.maximum(np.where(amax > 0, np.frexp(amax)[1] - 1 + 127, 0) - down, 1)
    scale = np.exp2(byte - 127.0)
    codes = (blocks / scale).astype(np.float32).astype(dtype).astype(np.float64)
    return np.moveaxis((codes * scale).reshape(v.shape), -1, axis)


WIDE = False


def mx_kscale(k):
    if not WIDE:
        return np.ones(k)
    levels = np.array([10, -10, 5, -5, 0])
    a = np.random.permutation(np.resize(levels, k // 512 * 4)).reshape(k // 512, 4)
    idx = np.arange(k)
    return np.exp2(a[idx // 512, idx % 128 // 32])


BF16 = ml_dtypes.bfloat16


def bf(x):
    return np.asarray(x, np.float32).astype(BF16)


def f64(x):
    return np.asarray(x).astype(np.float64)


B, IDIM, HDIM, ODIM, S, DEPTH, NACT, NTOP = 512, 8192, 1024, 512, 128, 32, 3, 2


def sigmoid(v):
    return 1.0 / (1.0 + np.exp(-v))


def setup_inputs():
    s, t = mx_kscale(IDIM), mx_kscale(HDIM)
    return {"x": bf(np.random.standard_normal((B, IDIM)) * s),
            "hidden": bf(np.random.standard_normal((B, HDIM)) * t),
            "stack_top": bf(np.random.standard_normal((B, NTOP, S))),
            "Wi": bf(np.random.standard_normal((HDIM, IDIM)) * 0.7 / np.sqrt(IDIM) / s),
            "bi": bf(np.random.standard_normal(HDIM) * 0.2),
            "Wh": bf(np.random.standard_normal((HDIM, HDIM)) * 0.7 / np.sqrt(HDIM) / t),
            "bh": bf(np.random.standard_normal(HDIM) * 0.2),
            "W0": bf(np.random.standard_normal((HDIM, S)) * 0.5 / np.sqrt(S)),
            "b0": bf(np.random.standard_normal(HDIM) * 0.2),
            "W1": bf(np.random.standard_normal((HDIM, S)) * 0.5 / np.sqrt(S)),
            "b1": bf(np.random.standard_normal(HDIM) * 0.2)}


def reference(x, hidden, stack_top, Wi, bi, Wh, bh, W0, b0, W1, b1):
    pre = ((mxq(f64(x), 1, "e4m3") @ mxq(f64(Wi), 1, "e4m3").T) + f64(bi)
           + (mxq(f64(hidden), 1, "e4m3") @ mxq(f64(Wh), 1, "e4m3").T) + f64(bh)
           + f64(stack_top)[:, 0] @ f64(W0).T + f64(b0)
           + f64(stack_top)[:, 1] @ f64(W1).T + f64(b1))
    return sigmoid(pre)

@@ -1,0 +1,188 @@
+from contextlib import ExitStack
+
+import concourse.mybir as mybir
+from concourse.masks import make_identity
+
+F32 = mybir.dt.float32
+BF16 = mybir.dt.bfloat16
+U32 = mybir.dt.uint32
+U8 = mybir.dt.uint8
+FP8X4 = mybir.dt.float8_e4m3fn_x4
+
+B, IDIM, HDIM, S = 512, 8192, 1024, 128
+P = 128
+K_PASS = 4 * P
+K_SPAN = 2 * K_PASS
+PASSES_PER_SPAN = K_SPAN // K_PASS
+PASSES = (IDIM + HDIM) // K_PASS
+ROWS = 512
+ROW_TILES = ROWS // P
+ROUNDS = HDIM // ROWS
+WORDS_PER_PASS = K_PASS // 2
+WORDS_PER_SPAN = K_SPAN // 2
+
+FLOPS = 2 * B * HDIM * (IDIM + HDIM + 2 * S)
+
+
+def tile_stackrnn_pa_k_kernel(tc, x, hidden, stack_top, Wi, bi, Wh, bh, W0, b0, W1, b1, out):
+    nc = tc.nc
+    with ExitStack() as ctx:
+        keep = ctx.enter_context(tc.tile_pool(name="keep", bufs=1))
+        act_raw_pool = ctx.enter_context(tc.tile_pool(name="act_raw", bufs=3))
+        wgt_raw_pool = ctx.enter_context(tc.tile_pool(name="wgt_raw", bufs=4))
+        grouped_pool = ctx.enter_context(tc.tile_pool(name="grouped", bufs=4))
+        wgt_mx_pool = ctx.enter_context(tc.tile_pool(name="wgt_mx", bufs=3))
+        result_pool = ctx.enter_context(tc.tile_pool(name="result", bufs=4))
+        work_psum = ctx.enter_context(tc.psum_pool(name="work_psum", bufs=4))
+        sum_psum = ctx.enter_context(tc.psum_pool(name="sum_psum", bufs=1))
+        ctx.enter_context(tc.manual_schedule())
+
+        st_raw = keep.tile([P, 4, 2, S], BF16)
+        nc.sync.dma_start(out=st_raw[:], in_=stack_top.rearrange("(p t) i s -> p t i s", t=4))
+        w01_raw = keep.tile([P, 2, 8, S], BF16)
+        nc.sync.dma_start(out=w01_raw[:, 0], in_=W0.rearrange("(p t) s -> p t s", t=8))
+        nc.sync.dma_start(out=w01_raw[:, 1], in_=W1.rearrange("(p t) s -> p t s", t=8))
+
+        bias_rows = keep.tile([P, HDIM], BF16)
+        nc.vector.memset(bias_rows[:], 0.0)
+        for row, bias in enumerate((bi, bh, b0, b1)):
+            nc.scalar.dma_start(out=bias_rows[row : row + 1, :], in_=bias.rearrange("(o n) -> o n", o=1))
+        ones = keep.tile([P, P], BF16)
+        nc.vector.memset(ones[:], 1.0)
+
+        ident_bf16 = keep.tile([P, P], BF16)
+        make_identity(nc, ident_bf16[:])
+        ident_f32 = keep.tile([P, P], F32)
+        make_identity(nc, ident_f32[:])
+
+        warm = keep.tile([P, 1], F32)
+        nc.vector.memset(warm[:], 0.0)
+        nc.scalar.activation(out=warm[:], in_=warm[:], func=mybir.ActivationFunctionType.Sigmoid)
+
+        st_bank = work_psum.tile([P, 4, 2, P], BF16, tag="work")
+        for t in range(4):
+            for i in range(2):
+                nc.tensor.transpose(out=st_bank[:, t, i, :], in_=st_raw[:, t, i, :], identity=ident_bf16[:])
+        st_T = keep.tile([P, 2, B], BF16)
+        nc.vector.tensor_copy(
+            out=st_T[:].rearrange("s i (p t) -> s i p t", t=4), in_=st_bank[:].rearrange("s t i p -> s i p t")
+        )
+        w01_T = keep.tile([P, 2, HDIM], BF16)
+        for i in range(2):
+            w_bank = work_psum.tile([P, 8, P], BF16, tag="work")
+            for t in range(8):
+                nc.tensor.transpose(out=w_bank[:, t, :], in_=w01_raw[:, i, t, :], identity=ident_bf16[:])
+            nc.scalar.copy(
+                out=w01_T[:, i, :].rearrange("s (p t) -> s p t", t=8), in_=w_bank[:].rearrange("s t p -> s p t")
+            )
+
+        bias_sum = keep.tile([P, HDIM], F32)
+        for rnd in range(ROUNDS):
+            cols = slice(rnd * ROWS, (rnd + 1) * ROWS)
+            bias_bank = work_psum.tile([P, ROWS], F32, tag="work")
+            nc.tensor.matmul(out=bias_bank[:], lhsT=ones[:], rhs=bias_rows[:, cols], start=True, stop=True)
+            nc.scalar.copy(out=bias_sum[:, cols], in_=bias_bank[:])
+
+        side = keep.tile([P, ROW_TILES, HDIM], F32)
+        for rnd in range(ROUNDS):
+            cols = slice(rnd * ROWS, (rnd + 1) * ROWS)
+            for bt in range(ROW_TILES):
+                rows = slice(bt * P, (bt + 1) * P)
+                stack_bank = work_psum.tile([P, ROWS], F32, tag="work")
+                for i in range(2):
+                    nc.tensor.matmul(
+                        out=stack_bank[:], lhsT=st_T[:, i, rows], rhs=w01_T[:, i, cols], start=(i == 0), stop=(i == 1)
+                    )
+                nc.vector.tensor_tensor(
+                    out=side[:, bt, cols], in0=stack_bank[:], in1=bias_sum[:, cols], op=mybir.AluOpType.add
+                )
+
+        act_codes = keep.tile([P, PASSES, B], U32, align_bytes=64)
+        act_scales = keep.tile([P, PASSES, B], U8, align_bytes=64)
+
+        def load_span(pool, first_pass, from_x, from_hidden, first_row):
+            k = first_pass * K_PASS
+            source, k = (from_x, k) if k < IDIM else (from_hidden, k - IDIM)
+            raw = pool.tile([P, ROW_TILES * K_SPAN], BF16, name="raw")
+            nc.sync.dma_start(
+                out=raw[:].rearrange("p (t k) -> p t k", t=ROW_TILES),
+                in_=source[first_row : first_row + ROWS, k : k + K_SPAN].rearrange("(t p) k -> p t k", p=P),
+            )
+            return raw
+
+        def transpose_pass(raw, which, first_bank_on_vector):
+            raw_words = raw[:].bitcast(F32)
+            grouped = grouped_pool.tile([P, 4 * ROWS], BF16, align_bytes=64)
+            grouped_words = grouped[:].bitcast(F32).rearrange("p (r u) -> p r u", u=2)
+            for half in range(2):
+                bank = work_psum.tile([P, 2, 2, P], F32, tag="work")
+                for a in range(2):
+                    for u in range(2):
+                        word = (2 * half + a) * WORDS_PER_SPAN + which * WORDS_PER_PASS + u * P
+                        nc.tensor.transpose(
+                            out=bank[:, a, u, :], in_=raw_words[:, word : word + P], identity=ident_f32[:]
+                        )
+                target = grouped_words[:, 2 * half * P : 2 * (half + 1) * P, :].rearrange("p (a r) u -> p a r u", a=2)
+                if first_bank_on_vector and half == 0:
+                    nc.vector.tensor_copy(out=target, in_=bank[:].rearrange("p a u r -> p a r u"))
+                else:
+                    nc.scalar.copy(out=target, in_=bank[:].rearrange("p a u r -> p a r u"))
+            return grouped
+
+        raw_now = {}
+
+        def prepare(rnd, passes):
+            wgt_codes = wgt_mx_pool.tile([P, len(passes), ROWS], U32, align_bytes=64)
+            wgt_scales = wgt_mx_pool.tile([P, len(passes), ROWS], U8, align_bytes=64)
+            todo = []
+            for n, c in enumerate(passes):
+                which = c % PASSES_PER_SPAN
+                if rnd == 0:
+                    if which == 0:
+                        raw_now["act"] = load_span(act_raw_pool, c, x, hidden, 0)
+                    grouped = transpose_pass(raw_now["act"], which, True)
+                    todo.append((grouped, act_codes[:, c, :], act_scales[:, c, :]))
+                if which == 0:
+                    raw_now["wgt"] = load_span(wgt_raw_pool, c, Wi, Wh, rnd * ROWS)
+                grouped = transpose_pass(raw_now["wgt"], which, rnd == 1 and n == 0)
+                todo.append((grouped, wgt_codes[:, n, :], wgt_scales[:, n, :]))
+            for grouped, codes, scales in todo:
+                nc.vector.quantize_mx(out=codes.bitcast(FP8X4), scales=scales, in_=grouped[:])
+            return wgt_codes, wgt_scales
+
+        def multiply(sums, passes, wgt_codes, wgt_scales):
+            for bt in range(ROW_TILES):
+                rows = slice(bt * P, (bt + 1) * P)
+                for n, c in enumerate(passes):
+                    nc.tensor.matmul_mx(
+                        out=sums[bt][:],
+                        lhsT=act_codes[:, c, rows].bitcast(FP8X4),
+                        lhsT_scale=act_scales[:, c, rows],
+                        rhs=wgt_codes[:, n, :].bitcast(FP8X4),
+                        rhs_scale=wgt_scales[:, n, :],
+                        start=(c == 0),
+                        stop=(c == PASSES - 1),
+                    )
+
+        def finish(rnd, sums):
+            cols = slice(rnd * ROWS, (rnd + 1) * ROWS)
+            for bt in range(ROW_TILES):
+                result = result_pool.tile([P, ROWS], F32)
+                nc.vector.tensor_tensor(out=result[:], in0=sums[bt][:], in1=side[:, bt, cols], op=mybir.AluOpType.add)
+                nc.scalar.activation(out=result[:], in_=result[:], func=mybir.ActivationFunctionType.Sigmoid)
+                nc.scalar.dma_start(out=out[bt * P : (bt + 1) * P, cols], in_=result[:])
+
+        steps = [(0, [c]) for c in range(PASSES)] + [(1, [c, c + 1]) for c in range(0, PASSES, 2)]
+
+        sums = {}
+        waiting = None
+        for step in steps + [None]:
+            operands = prepare(step[0], step[1]) if step is not None else None
+            if waiting is not None:
+                (rnd, passes), (wgt_codes, wgt_scales) = waiting
+                if passes[0] == 0:
+                    sums[rnd] = [sum_psum.tile([P, ROWS], F32, name="sum%d" % bt) for bt in range(ROW_TILES)]
+                multiply(sums[rnd], passes, wgt_codes, wgt_scales)
+                if passes[-1] == PASSES - 1:
+                    finish(rnd, sums[rnd])
+            waiting = (step, operands)

@@ -20,6 +20,10 @@ ROW_TILES = ROWS // P
 ROUNDS = HDIM // ROWS
 WORDS_PER_PASS = K_PASS // 2
 WORDS_PER_SPAN = K_SPAN // 2
+SPANS = PASSES // PASSES_PER_SPAN
+TRANSPOSES_PER_PASS = 2 * ROW_TILES
+TRANSPOSES_PER_BANK = 4
+TRANSPOSES_PER_RUN = 32
 
 FLOPS = 2 * B * HDIM * (IDIM + HDIM + 2 * S)
 
@@ -30,9 +34,9 @@ def tile_stackrnn_pa_k_kernel(tc, x, hidden, stack_top, Wi, bi, Wh, bh, W0, b0, 
         keep = ctx.enter_context(tc.tile_pool(name="keep", bufs=1))
         act_raw_pool = ctx.enter_context(tc.tile_pool(name="act_raw", bufs=3))
         wgt_raw_pool = ctx.enter_context(tc.tile_pool(name="wgt_raw", bufs=4))
-        grouped_pool = ctx.enter_context(tc.tile_pool(name="grouped", bufs=4))
-        wgt_mx_pool = ctx.enter_context(tc.tile_pool(name="wgt_mx", bufs=3))
-        result_pool = ctx.enter_context(tc.tile_pool(name="result", bufs=4))
+        grouped_pool = ctx.enter_context(tc.tile_pool(name="grouped", bufs=6))
+        wgt_mx_pool = ctx.enter_context(tc.tile_pool(name="wgt_mx", bufs=2))
+        result_pool = ctx.enter_context(tc.tile_pool(name="result", bufs=ROUNDS * ROW_TILES))
         work_psum = ctx.enter_context(tc.psum_pool(name="work_psum", bufs=4))
         sum_psum = ctx.enter_context(tc.psum_pool(name="sum_psum", bufs=1))
         ctx.enter_context(tc.manual_schedule())
@@ -42,6 +46,24 @@ def tile_stackrnn_pa_k_kernel(tc, x, hidden, stack_top, Wi, bi, Wh, bh, W0, b0, 
         w01_raw = keep.tile([P, 2, 8, S], BF16)
         nc.sync.dma_start(out=w01_raw[:, 0], in_=W0.rearrange("(p t) s -> p t s", t=8))
         nc.sync.dma_start(out=w01_raw[:, 1], in_=W1.rearrange("(p t) s -> p t s", t=8))
+
+        def load_span(pool, span, from_x, from_hidden, first_row):
+            k = span * K_SPAN
+            source, k = (from_x, k) if k < IDIM else (from_hidden, k - IDIM)
+            raw = pool.tile([P, ROW_TILES * K_SPAN], BF16, name="raw")
+            nc.sync.dma_start(
+                out=raw[:].rearrange("p (t k) -> p t k", t=ROW_TILES),
+                in_=source[first_row : first_row + ROWS, k : k + K_SPAN].rearrange("(t p) k -> p t k", p=P),
+            )
+            return raw
+
+        act_raw = {}
+        wgt_raw = {}
+        for rnd in range(ROUNDS):
+            for span in range(SPANS):
+                if rnd == 0:
+                    act_raw[span] = load_span(act_raw_pool, span, x, hidden, 0)
+                wgt_raw[(rnd, span)] = load_span(wgt_raw_pool, span, Wi, Wh, rnd * ROWS)
 
         bias_rows = keep.tile([P, HDIM], BF16)
         nc.vector.memset(bias_rows[:], 0.0)
@@ -72,9 +94,8 @@ def tile_stackrnn_pa_k_kernel(tc, x, hidden, stack_top, Wi, bi, Wh, bh, W0, b0, 
             w_bank = work_psum.tile([P, 8, P], BF16, tag="work")
             for t in range(8):
                 nc.tensor.transpose(out=w_bank[:, t, :], in_=w01_raw[:, i, t, :], identity=ident_bf16[:])
-            nc.scalar.copy(
-                out=w01_T[:, i, :].rearrange("s (p t) -> s p t", t=8), in_=w_bank[:].rearrange("s t p -> s p t")
-            )
+            copy_out = nc.scalar.copy if i == 0 else nc.vector.tensor_copy
+            copy_out(out=w01_T[:, i, :].rearrange("s (p t) -> s p t", t=8), in_=w_bank[:].rearrange("s t p -> s p t"))
 
         bias_sum = keep.tile([P, HDIM], F32)
         for rnd in range(ROUNDS):
@@ -100,21 +121,11 @@ def tile_stackrnn_pa_k_kernel(tc, x, hidden, stack_top, Wi, bi, Wh, bh, W0, b0, 
         act_codes = keep.tile([P, PASSES, B], U32, align_bytes=64)
         act_scales = keep.tile([P, PASSES, B], U8, align_bytes=64)
 
-        def load_span(pool, first_pass, from_x, from_hidden, first_row):
-            k = first_pass * K_PASS
-            source, k = (from_x, k) if k < IDIM else (from_hidden, k - IDIM)
-            raw = pool.tile([P, ROW_TILES * K_SPAN], BF16, name="raw")
-            nc.sync.dma_start(
-                out=raw[:].rearrange("p (t k) -> p t k", t=ROW_TILES),
-                in_=source[first_row : first_row + ROWS, k : k + K_SPAN].rearrange("(t p) k -> p t k", p=P),
-            )
-            return raw
-
-        def transpose_pass(raw, which, first_bank_on_vector):
+        def transpose_pass(raw, which, last_bank_on_vector):
             raw_words = raw[:].bitcast(F32)
             grouped = grouped_pool.tile([P, 4 * ROWS], BF16, align_bytes=64)
             grouped_words = grouped[:].bitcast(F32).rearrange("p (r u) -> p r u", u=2)
-            for half in range(2):
+            for half in range(TRANSPOSES_PER_PASS // TRANSPOSES_PER_BANK):
                 bank = work_psum.tile([P, 2, 2, P], F32, tag="work")
                 for a in range(2):
                     for u in range(2):
@@ -123,31 +134,24 @@ def tile_stackrnn_pa_k_kernel(tc, x, hidden, stack_top, Wi, bi, Wh, bh, W0, b0, 
                             out=bank[:, a, u, :], in_=raw_words[:, word : word + P], identity=ident_f32[:]
                         )
                 target = grouped_words[:, 2 * half * P : 2 * (half + 1) * P, :].rearrange("p (a r) u -> p a r u", a=2)
-                if first_bank_on_vector and half == 0:
+                if last_bank_on_vector and half == 1:
                     nc.vector.tensor_copy(out=target, in_=bank[:].rearrange("p a u r -> p a r u"))
                 else:
                     nc.scalar.copy(out=target, in_=bank[:].rearrange("p a u r -> p a r u"))
             return grouped
 
-        raw_now = {}
-
         def prepare(rnd, passes):
             wgt_codes = wgt_mx_pool.tile([P, len(passes), ROWS], U32, align_bytes=64)
             wgt_scales = wgt_mx_pool.tile([P, len(passes), ROWS], U8, align_bytes=64)
-            todo = []
+            jobs = []
             for n, c in enumerate(passes):
-                which = c % PASSES_PER_SPAN
+                span, which = divmod(c, PASSES_PER_SPAN)
                 if rnd == 0:
-                    if which == 0:
-                        raw_now["act"] = load_span(act_raw_pool, c, x, hidden, 0)
-                    grouped = transpose_pass(raw_now["act"], which, True)
-                    todo.append((grouped, act_codes[:, c, :], act_scales[:, c, :]))
-                if which == 0:
-                    raw_now["wgt"] = load_span(wgt_raw_pool, c, Wi, Wh, rnd * ROWS)
-                grouped = transpose_pass(raw_now["wgt"], which, rnd == 1 and n == 0)
-                todo.append((grouped, wgt_codes[:, n, :], wgt_scales[:, n, :]))
-            for grouped, codes, scales in todo:
-                nc.vector.quantize_mx(out=codes.bitcast(FP8X4), scales=scales, in_=grouped[:])
+                    jobs.append((act_raw[span], which, act_codes[:, c, :], act_scales[:, c, :]))
+                jobs.append((wgt_raw[(rnd, span)], which, wgt_codes[:, n, :], wgt_scales[:, n, :]))
+            grouped = [transpose_pass(raw, which, j % 2 == 1) for j, (raw, which, codes, scales) in enumerate(jobs)]
+            for (raw, which, codes, scales), values in zip(jobs, grouped):
+                nc.vector.quantize_mx(out=codes.bitcast(FP8X4), scales=scales, in_=values[:])
             return wgt_codes, wgt_scales
 
         def multiply(sums, passes, wgt_codes, wgt_scales):
@@ -170,14 +174,19 @@ def tile_stackrnn_pa_k_kernel(tc, x, hidden, stack_top, Wi, bi, Wh, bh, W0, b0, 
                 result = result_pool.tile([P, ROWS], F32)
                 nc.vector.tensor_tensor(out=result[:], in0=sums[bt][:], in1=side[:, bt, cols], op=mybir.AluOpType.add)
                 nc.scalar.activation(out=result[:], in_=result[:], func=mybir.ActivationFunctionType.Sigmoid)
-                nc.scalar.dma_start(out=out[bt * P : (bt + 1) * P, cols], in_=result[:])
+                nc.sync.dma_start(out=out[bt * P : (bt + 1) * P, cols], in_=result[:])
 
-        steps = [(0, [c]) for c in range(PASSES)] + [(1, [c, c + 1]) for c in range(0, PASSES, 2)]
+        steps = []
+        for rnd in range(ROUNDS):
+            operands_to_make = 2 if rnd == 0 else 1
+            passes_per_step = TRANSPOSES_PER_RUN // (operands_to_make * TRANSPOSES_PER_PASS)
+            for first in range(0, PASSES, passes_per_step):
+                steps.append((rnd, list(range(first, min(first + passes_per_step, PASSES)))))
 
         sums = {}
         waiting = None
         for step in steps + [None]:
-            operands = prepare(step[0], step[1]) if step is not None else None
+            prepared = prepare(step[0], step[1]) if step is not None else None
             if waiting is not None:
                 (rnd, passes), (wgt_codes, wgt_scales) = waiting
                 if passes[0] == 0:
@@ -185,4 +194,4 @@ def tile_stackrnn_pa_k_kernel(tc, x, hidden, stack_top, Wi, bi, Wh, bh, W0, b0, 
                 multiply(sums[rnd], passes, wgt_codes, wgt_scales)
                 if passes[-1] == PASSES - 1:
                     finish(rnd, sums[rnd])
-            waiting = (step, operands)
+            waiting = (step, prepared)

@@ -23,7 +23,7 @@ WORDS_PER_SPAN = K_SPAN // 2
 SPANS = PASSES // PASSES_PER_SPAN
 TRANSPOSES_PER_PASS = 2 * ROW_TILES
 TRANSPOSES_PER_BANK = 4
-TRANSPOSES_PER_RUN = 32
+TRANSPOSES_PER_RUN = 16
 
 FLOPS = 2 * B * HDIM * (IDIM + HDIM + 2 * S)
 

@@ -19,10 +19,10 @@ ROWS = 512
 ROW_TILES = ROWS // P
 ROUNDS = HDIM // ROWS
 WORDS_PER_PASS = K_PASS // 2
-WORDS_PER_SPAN = K_SPAN // 2
 SPANS = PASSES // PASSES_PER_SPAN
 TRANSPOSES_PER_PASS = 2 * ROW_TILES
 TRANSPOSES_PER_BANK = 4
+WARM_UP_MATMULS = 5
 TRANSPOSES_PER_RUN = 16
 
 FLOPS = 2 * B * HDIM * (IDIM + HDIM + 2 * S)
@@ -47,23 +47,46 @@ def tile_stackrnn_pa_k_kernel(tc, x, hidden, stack_top, Wi, bi, Wh, bh, W0, b0, 
         nc.sync.dma_start(out=w01_raw[:, 0], in_=W0.rearrange("(p t) s -> p t s", t=8))
         nc.sync.dma_start(out=w01_raw[:, 1], in_=W1.rearrange("(p t) s -> p t s", t=8))
 
-        def load_span(pool, span, from_x, from_hidden, first_row):
+        def load_span(pool, span, from_x, from_hidden, first_row, passes_per_load):
             k = span * K_SPAN
             source, k = (from_x, k) if k < IDIM else (from_hidden, k - IDIM)
             raw = pool.tile([P, ROW_TILES * K_SPAN], BF16, name="raw")
-            nc.sync.dma_start(
-                out=raw[:].rearrange("p (t k) -> p t k", t=ROW_TILES),
-                in_=source[first_row : first_row + ROWS, k : k + K_SPAN].rearrange("(t p) k -> p t k", p=P),
-            )
-            return raw
+            width = passes_per_load * K_PASS
+            words = []
+            loads = []
+            for first in range(0, PASSES_PER_SPAN, passes_per_load):
+                start = first * ROW_TILES * K_PASS
+                loads.append(
+                    (
+                        raw[:, start : start + ROW_TILES * width].rearrange("p (t k) -> p t k", t=ROW_TILES),
+                        source[
+                            first_row : first_row + ROWS, k + first * K_PASS : k + first * K_PASS + width
+                        ].rearrange("(t p) k -> p t k", p=P),
+                    )
+                )
+                words += [(raw, width // 2, start // 2 + n * WORDS_PER_PASS) for n in range(passes_per_load)]
+            return words, loads
 
         act_raw = {}
         wgt_raw = {}
         for rnd in range(ROUNDS):
             for span in range(SPANS):
+                passes_per_load = 1 if (rnd, span) == (0, 0) else PASSES_PER_SPAN
+                loads = []
                 if rnd == 0:
-                    act_raw[span] = load_span(act_raw_pool, span, x, hidden, 0)
-                wgt_raw[(rnd, span)] = load_span(wgt_raw_pool, span, Wi, Wh, rnd * ROWS)
+                    act_raw[span], act_loads = load_span(act_raw_pool, span, x, hidden, 0, passes_per_load)
+                    loads.append(act_loads)
+                wgt_raw[(rnd, span)], wgt_loads = load_span(wgt_raw_pool, span, Wi, Wh, rnd * ROWS, passes_per_load)
+                loads.append(wgt_loads)
+                for together in zip(*loads):
+                    for target, source in together:
+                        nc.sync.dma_start(out=target, in_=source)
+
+        zeros = keep.tile([P, ROWS], BF16)
+        nc.vector.memset(zeros[:], 0.0)
+        warm_bank = work_psum.tile([P, ROWS], F32, tag="work")
+        for n in range(WARM_UP_MATMULS):
+            nc.tensor.matmul(out=warm_bank[:], lhsT=zeros[:, :P], rhs=zeros[:], start=True, stop=True)
 
         bias_rows = keep.tile([P, HDIM], BF16)
         nc.vector.memset(bias_rows[:], 0.0)
@@ -105,7 +128,8 @@ def tile_stackrnn_pa_k_kernel(tc, x, hidden, stack_top, Wi, bi, Wh, bh, W0, b0, 
             nc.scalar.copy(out=bias_sum[:, cols], in_=bias_bank[:])
 
         side = keep.tile([P, ROW_TILES, HDIM], F32)
-        for rnd in range(ROUNDS):
+
+        def make_side(rnd):
             cols = slice(rnd * ROWS, (rnd + 1) * ROWS)
             for bt in range(ROW_TILES):
                 rows = slice(bt * P, (bt + 1) * P)
@@ -121,7 +145,7 @@ def tile_stackrnn_pa_k_kernel(tc, x, hidden, stack_top, Wi, bi, Wh, bh, W0, b0, 
         act_codes = keep.tile([P, PASSES, B], U32, align_bytes=64)
         act_scales = keep.tile([P, PASSES, B], U8, align_bytes=64)
 
-        def transpose_pass(raw, which, last_bank_on_vector):
+        def transpose_pass(raw, run_pitch, first_word, last_bank_on_vector):
             raw_words = raw[:].bitcast(F32)
             grouped = grouped_pool.tile([P, 4 * ROWS], BF16, align_bytes=64)
             grouped_words = grouped[:].bitcast(F32).rearrange("p (r u) -> p r u", u=2)
@@ -129,7 +153,7 @@ def tile_stackrnn_pa_k_kernel(tc, x, hidden, stack_top, Wi, bi, Wh, bh, W0, b0, 
                 bank = work_psum.tile([P, 2, 2, P], F32, tag="work")
                 for a in range(2):
                     for u in range(2):
-                        word = (2 * half + a) * WORDS_PER_SPAN + which * WORDS_PER_PASS + u * P
+                        word = (2 * half + a) * run_pitch + first_word + u * P
                         nc.tensor.transpose(
                             out=bank[:, a, u, :], in_=raw_words[:, word : word + P], identity=ident_f32[:]
                         )
@@ -147,10 +171,10 @@ def tile_stackrnn_pa_k_kernel(tc, x, hidden, stack_top, Wi, bi, Wh, bh, W0, b0, 
             for n, c in enumerate(passes):
                 span, which = divmod(c, PASSES_PER_SPAN)
                 if rnd == 0:
-                    jobs.append((act_raw[span], which, act_codes[:, c, :], act_scales[:, c, :]))
-                jobs.append((wgt_raw[(rnd, span)], which, wgt_codes[:, n, :], wgt_scales[:, n, :]))
-            grouped = [transpose_pass(raw, which, j % 2 == 1) for j, (raw, which, codes, scales) in enumerate(jobs)]
-            for (raw, which, codes, scales), values in zip(jobs, grouped):
+                    jobs.append((act_raw[span][which], act_codes[:, c, :], act_scales[:, c, :]))
+                jobs.append((wgt_raw[(rnd, span)][which], wgt_codes[:, n, :], wgt_scales[:, n, :]))
+            grouped = [transpose_pass(*words, j % 2 == 1) for j, (words, codes, scales) in enumerate(jobs)]
+            for (words, codes, scales), values in zip(jobs, grouped):
                 nc.vector.quantize_mx(out=codes.bitcast(FP8X4), scales=scales, in_=values[:])
             return wgt_codes, wgt_scales
 
@@ -168,11 +192,18 @@ def tile_stackrnn_pa_k_kernel(tc, x, hidden, stack_top, Wi, bi, Wh, bh, W0, b0, 
                         stop=(c == PASSES - 1),
                     )
 
-        def finish(rnd, sums):
+        def add_side(rnd, sums):
             cols = slice(rnd * ROWS, (rnd + 1) * ROWS)
+            results = []
             for bt in range(ROW_TILES):
-                result = result_pool.tile([P, ROWS], F32)
+                result = result_pool.tile([P, ROWS], F32, name="result")
                 nc.vector.tensor_tensor(out=result[:], in0=sums[bt][:], in1=side[:, bt, cols], op=mybir.AluOpType.add)
+                results.append(result)
+            return results
+
+        def store(rnd, results):
+            cols = slice(rnd * ROWS, (rnd + 1) * ROWS)
+            for bt, result in enumerate(results):
                 nc.scalar.activation(out=result[:], in_=result[:], func=mybir.ActivationFunctionType.Sigmoid)
                 nc.sync.dma_start(out=out[bt * P : (bt + 1) * P, cols], in_=result[:])
 
@@ -185,13 +216,21 @@ def tile_stackrnn_pa_k_kernel(tc, x, hidden, stack_top, Wi, bi, Wh, bh, W0, b0, 
 
         sums = {}
         waiting = None
+        unstored = None
+        make_side(0)
         for step in steps + [None]:
             prepared = prepare(step[0], step[1]) if step is not None else None
+            if step == steps[0]:
+                make_side(1)
             if waiting is not None:
                 (rnd, passes), (wgt_codes, wgt_scales) = waiting
                 if passes[0] == 0:
                     sums[rnd] = [sum_psum.tile([P, ROWS], F32, name="sum%d" % bt) for bt in range(ROW_TILES)]
                 multiply(sums[rnd], passes, wgt_codes, wgt_scales)
+                if unstored is not None:
+                    store(*unstored)
+                    unstored = None
                 if passes[-1] == PASSES - 1:
-                    finish(rnd, sums[rnd])
+                    unstored = (rnd, add_side(rnd, sums[rnd]))
             waiting = (step, prepared)
+        store(*unstored)

@@ -23,6 +23,7 @@ SPANS = PASSES // PASSES_PER_SPAN
 TRANSPOSES_PER_PASS = 2 * ROW_TILES
 TRANSPOSES_PER_BANK = 4
 WARM_UP_MATMULS = 5
+SIDE_BANKS = {0: 1, 1: 2, 2: 2, 3: 2, 4: 1}
 TRANSPOSES_PER_RUN = 16
 
 FLOPS = 2 * B * HDIM * (IDIM + HDIM + 2 * S)
@@ -42,10 +43,13 @@ def tile_stackrnn_pa_k_kernel(tc, x, hidden, stack_top, Wi, bi, Wh, bh, W0, b0, 
         ctx.enter_context(tc.manual_schedule())
 
         st_raw = keep.tile([P, 4, 2, S], BF16)
-        nc.sync.dma_start(out=st_raw[:], in_=stack_top.rearrange("(p t) i s -> p t i s", t=4))
+        st_raw = keep.tile([P, 4, 2, S], BF16)
         w01_raw = keep.tile([P, 2, 8, S], BF16)
-        nc.sync.dma_start(out=w01_raw[:, 0], in_=W0.rearrange("(p t) s -> p t s", t=8))
-        nc.sync.dma_start(out=w01_raw[:, 1], in_=W1.rearrange("(p t) s -> p t s", t=8))
+
+        def load_small():
+            nc.sync.dma_start(out=st_raw[:], in_=stack_top.rearrange("(p t) i s -> p t i s", t=4))
+            nc.sync.dma_start(out=w01_raw[:, 0], in_=W0.rearrange("(p t) s -> p t s", t=8))
+            nc.sync.dma_start(out=w01_raw[:, 1], in_=W1.rearrange("(p t) s -> p t s", t=8))
 
         def load_span(pool, span, from_x, from_hidden, first_row, passes_per_load):
             k = span * K_SPAN
@@ -69,6 +73,7 @@ def tile_stackrnn_pa_k_kernel(tc, x, hidden, stack_top, Wi, bi, Wh, bh, W0, b0, 
 
         act_raw = {}
         wgt_raw = {}
+        load_small()
         for rnd in range(ROUNDS):
             for span in range(SPANS):
                 passes_per_load = 1 if (rnd, span) == (0, 0) else PASSES_PER_SPAN
@@ -83,13 +88,13 @@ def tile_stackrnn_pa_k_kernel(tc, x, hidden, stack_top, Wi, bi, Wh, bh, W0, b0, 
                         nc.sync.dma_start(out=target, in_=source)
 
         zeros = keep.tile([P, ROWS], BF16)
-        nc.vector.memset(zeros[:], 0.0)
+        nc.gpsimd.memset(zeros[:].bitcast(F32), 0.0)
         warm_bank = work_psum.tile([P, ROWS], F32, tag="work")
         for n in range(WARM_UP_MATMULS):
             nc.tensor.matmul(out=warm_bank[:], lhsT=zeros[:, :P], rhs=zeros[:], start=True, stop=True)
 
         bias_rows = keep.tile([P, HDIM], BF16)
-        nc.vector.memset(bias_rows[:], 0.0)
+        nc.vector.memset(bias_rows[:].bitcast(F32), 0.0)
         for row, bias in enumerate((bi, bh, b0, b1)):
             nc.scalar.dma_start(out=bias_rows[row : row + 1, :], in_=bias.rearrange("(o n) -> o n", o=1))
         ones = keep.tile([P, P], BF16)
@@ -104,43 +109,45 @@ def tile_stackrnn_pa_k_kernel(tc, x, hidden, stack_top, Wi, bi, Wh, bh, W0, b0, 
         nc.vector.memset(warm[:], 0.0)
         nc.scalar.activation(out=warm[:], in_=warm[:], func=mybir.ActivationFunctionType.Sigmoid)
 
-        st_bank = work_psum.tile([P, 4, 2, P], BF16, tag="work")
-        for t in range(4):
-            for i in range(2):
-                nc.tensor.transpose(out=st_bank[:, t, i, :], in_=st_raw[:, t, i, :], identity=ident_bf16[:])
         st_T = keep.tile([P, 2, B], BF16)
-        nc.vector.tensor_copy(
-            out=st_T[:].rearrange("s i (p t) -> s i p t", t=4), in_=st_bank[:].rearrange("s t i p -> s i p t")
-        )
         w01_T = keep.tile([P, 2, HDIM], BF16)
-        for i in range(2):
-            w_bank = work_psum.tile([P, 8, P], BF16, tag="work")
-            for t in range(8):
-                nc.tensor.transpose(out=w_bank[:, t, :], in_=w01_raw[:, i, t, :], identity=ident_bf16[:])
-            copy_out = nc.scalar.copy if i == 0 else nc.vector.tensor_copy
-            copy_out(out=w01_T[:, i, :].rearrange("s (p t) -> s p t", t=8), in_=w_bank[:].rearrange("s t p -> s p t"))
-
         bias_sum = keep.tile([P, HDIM], F32)
-        for rnd in range(ROUNDS):
-            cols = slice(rnd * ROWS, (rnd + 1) * ROWS)
-            bias_bank = work_psum.tile([P, ROWS], F32, tag="work")
-            nc.tensor.matmul(out=bias_bank[:], lhsT=ones[:], rhs=bias_rows[:, cols], start=True, stop=True)
-            nc.scalar.copy(out=bias_sum[:, cols], in_=bias_bank[:])
+
+        def prepare_side():
+            st_bank = work_psum.tile([P, 4, 2, P], BF16, tag="work")
+            for t in range(4):
+                for i in range(2):
+                    nc.tensor.transpose(out=st_bank[:, t, i, :], in_=st_raw[:, t, i, :], identity=ident_bf16[:])
+            nc.vector.tensor_copy(
+                out=st_T[:].rearrange("s i (p t) -> s i p t", t=4), in_=st_bank[:].rearrange("s t i p -> s i p t")
+            )
+            for i in range(2):
+                w_bank = work_psum.tile([P, 8, P], BF16, tag="work")
+                for t in range(8):
+                    nc.tensor.transpose(out=w_bank[:, t, :], in_=w01_raw[:, i, t, :], identity=ident_bf16[:])
+                copy_out = nc.scalar.copy if i == 0 else nc.vector.tensor_copy
+                copy_out(out=w01_T[:, i, :].rearrange("s (p t) -> s p t", t=8), in_=w_bank[:].rearrange("s t p -> s p t"))
+
+            for rnd in range(ROUNDS):
+                cols = slice(rnd * ROWS, (rnd + 1) * ROWS)
+                bias_bank = work_psum.tile([P, ROWS], F32, tag="work")
+                nc.tensor.matmul(out=bias_bank[:], lhsT=ones[:], rhs=bias_rows[:, cols], start=True, stop=True)
+                nc.scalar.copy(out=bias_sum[:, cols], in_=bias_bank[:])
+
 
         side = keep.tile([P, ROW_TILES, HDIM], F32)
 
-        def make_side(rnd):
+        def make_side(rnd, bt):
             cols = slice(rnd * ROWS, (rnd + 1) * ROWS)
-            for bt in range(ROW_TILES):
-                rows = slice(bt * P, (bt + 1) * P)
-                stack_bank = work_psum.tile([P, ROWS], F32, tag="work")
-                for i in range(2):
-                    nc.tensor.matmul(
-                        out=stack_bank[:], lhsT=st_T[:, i, rows], rhs=w01_T[:, i, cols], start=(i == 0), stop=(i == 1)
-                    )
-                nc.vector.tensor_tensor(
-                    out=side[:, bt, cols], in0=stack_bank[:], in1=bias_sum[:, cols], op=mybir.AluOpType.add
+            rows = slice(bt * P, (bt + 1) * P)
+            stack_bank = work_psum.tile([P, ROWS], F32, tag="work")
+            for i in range(2):
+                nc.tensor.matmul(
+                    out=stack_bank[:], lhsT=st_T[:, i, rows], rhs=w01_T[:, i, cols], start=(i == 0), stop=(i == 1)
                 )
+            nc.vector.tensor_tensor(
+                out=side[:, bt, cols], in0=stack_bank[:], in1=bias_sum[:, cols], op=mybir.AluOpType.add
+            )
 
         act_codes = keep.tile([P, PASSES, B], U32, align_bytes=64)
         act_scales = keep.tile([P, PASSES, B], U8, align_bytes=64)
@@ -192,20 +199,34 @@ def tile_stackrnn_pa_k_kernel(tc, x, hidden, stack_top, Wi, bi, Wh, bh, W0, b0, 
                         stop=(c == PASSES - 1),
                     )
 
+        def pieces_of(rnd, bt):
+            n = 2 if rnd == ROUNDS - 1 and bt == ROW_TILES - 1 else 1
+            return [slice(i * ROWS // n, (i + 1) * ROWS // n) for i in range(n)]
+
         def add_side(rnd, sums):
-            cols = slice(rnd * ROWS, (rnd + 1) * ROWS)
             results = []
             for bt in range(ROW_TILES):
                 result = result_pool.tile([P, ROWS], F32, name="result")
-                nc.vector.tensor_tensor(out=result[:], in0=sums[bt][:], in1=side[:, bt, cols], op=mybir.AluOpType.add)
+                for cols in pieces_of(rnd, bt):
+                    nc.vector.tensor_tensor(
+                        out=result[:, cols],
+                        in0=sums[bt][:, cols],
+                        in1=side[:, bt, rnd * ROWS + cols.start : rnd * ROWS + cols.stop],
+                        op=mybir.AluOpType.add,
+                    )
                 results.append(result)
             return results
 
         def store(rnd, results):
-            cols = slice(rnd * ROWS, (rnd + 1) * ROWS)
             for bt, result in enumerate(results):
-                nc.scalar.activation(out=result[:], in_=result[:], func=mybir.ActivationFunctionType.Sigmoid)
-                nc.sync.dma_start(out=out[bt * P : (bt + 1) * P, cols], in_=result[:])
+                for cols in pieces_of(rnd, bt):
+                    nc.scalar.activation(
+                        out=result[:, cols], in_=result[:, cols], func=mybir.ActivationFunctionType.Sigmoid
+                    )
+                    nc.sync.dma_start(
+                        out=out[bt * P : (bt + 1) * P, rnd * ROWS + cols.start : rnd * ROWS + cols.stop],
+                        in_=result[:, cols],
+                    )
 
         steps = []
         for rnd in range(ROUNDS):
@@ -217,11 +238,12 @@ def tile_stackrnn_pa_k_kernel(tc, x, hidden, stack_top, Wi, bi, Wh, bh, W0, b0, 
         sums = {}
         waiting = None
         unstored = None
-        make_side(0)
+        banks_of_side = [(rnd, bt) for rnd in range(ROUNDS) for bt in range(ROW_TILES)]
+        prepare_side()
         for step in steps + [None]:
+            for n in range(SIDE_BANKS.get(steps.index(step), 0) if step is not None else 0):
+                make_side(*banks_of_side.pop(0))
             prepared = prepare(step[0], step[1]) if step is not None else None
-            if step == steps[0]:
-                make_side(1)
             if waiting is not None:
                 (rnd, passes), (wgt_codes, wgt_scales) = waiting
                 if passes[0] == 0:

@@ -90,8 +90,12 @@ def tile_stackrnn_pa_k_kernel(tc, x, hidden, stack_top, Wi, bi, Wh, bh, W0, b0, 
         zeros = keep.tile([P, ROWS], BF16)
         nc.gpsimd.memset(zeros[:].bitcast(F32), 0.0)
         warm_bank = work_psum.tile([P, ROWS], F32, tag="work")
-        for n in range(WARM_UP_MATMULS):
-            nc.tensor.matmul(out=warm_bank[:], lhsT=zeros[:, :P], rhs=zeros[:], start=True, stop=True)
+
+        def warm_up(matmuls):
+            for n in range(matmuls):
+                nc.tensor.matmul(out=warm_bank[:], lhsT=zeros[:, :P], rhs=zeros[:], start=True, stop=True)
+
+        warm_up(WARM_UP_MATMULS)
 
         bias_rows = keep.tile([P, HDIM], BF16)
         nc.vector.memset(bias_rows[:].bitcast(F32), 0.0)
@@ -121,6 +125,7 @@ def tile_stackrnn_pa_k_kernel(tc, x, hidden, stack_top, Wi, bi, Wh, bh, W0, b0, 
             nc.vector.tensor_copy(
                 out=st_T[:].rearrange("s i (p t) -> s i p t", t=4), in_=st_bank[:].rearrange("s t i p -> s i p t")
             )
+            warm_up(2)
             for i in range(2):
                 w_bank = work_psum.tile([P, 8, P], BF16, tag="work")
                 for t in range(8):
@@ -152,7 +157,7 @@ def tile_stackrnn_pa_k_kernel(tc, x, hidden, stack_top, Wi, bi, Wh, bh, W0, b0, 
         act_codes = keep.tile([P, PASSES, B], U32, align_bytes=64)
         act_scales = keep.tile([P, PASSES, B], U8, align_bytes=64)
 
-        def transpose_pass(raw, run_pitch, first_word, last_bank_on_vector):
+        def transpose_pass(raw, run_pitch, first_word, third_bank_on_vector):
             raw_words = raw[:].bitcast(F32)
             grouped = grouped_pool.tile([P, 4 * ROWS], BF16, align_bytes=64)
             grouped_words = grouped[:].bitcast(F32).rearrange("p (r u) -> p r u", u=2)
@@ -165,7 +170,7 @@ def tile_stackrnn_pa_k_kernel(tc, x, hidden, stack_top, Wi, bi, Wh, bh, W0, b0, 
                             out=bank[:, a, u, :], in_=raw_words[:, word : word + P], identity=ident_f32[:]
                         )
                 target = grouped_words[:, 2 * half * P : 2 * (half + 1) * P, :].rearrange("p (a r) u -> p a r u", a=2)
-                if last_bank_on_vector and half == 1:
+                if third_bank_on_vector and half == 0:
                     nc.vector.tensor_copy(out=target, in_=bank[:].rearrange("p a u r -> p a r u"))
                 else:
                     nc.scalar.copy(out=target, in_=bank[:].rearrange("p a u r -> p a r u"))

@@ -23,7 +23,6 @@ SPANS = PASSES // PASSES_PER_SPAN
 TRANSPOSES_PER_PASS = 2 * ROW_TILES
 TRANSPOSES_PER_BANK = 4
 WARM_UP_MATMULS = 5
-SIDE_BANKS = {0: 1, 1: 2, 2: 2, 3: 2, 4: 1}
 TRANSPOSES_PER_RUN = 16
 
 FLOPS = 2 * B * HDIM * (IDIM + HDIM + 2 * S)
@@ -142,22 +141,28 @@ def tile_stackrnn_pa_k_kernel(tc, x, hidden, stack_top, Wi, bi, Wh, bh, W0, b0, 
 
         side = keep.tile([P, ROW_TILES, HDIM], F32)
 
-        def make_side(rnd, bt):
+        def side_pieces(rnd, bt):
             cols = slice(rnd * ROWS, (rnd + 1) * ROWS)
             rows = slice(bt * P, (bt + 1) * P)
-            stack_bank = work_psum.tile([P, ROWS], F32, tag="work")
-            for i in range(2):
+            banks = []
+
+            def multiply_stack(i):
+                if i == 0:
+                    banks.append(work_psum.tile([P, ROWS], F32, tag="work", name="stack_bank"))
                 nc.tensor.matmul(
-                    out=stack_bank[:], lhsT=st_T[:, i, rows], rhs=w01_T[:, i, cols], start=(i == 0), stop=(i == 1)
+                    out=banks[0][:], lhsT=st_T[:, i, rows], rhs=w01_T[:, i, cols], start=(i == 0), stop=(i == 1)
                 )
-            nc.vector.tensor_tensor(
-                out=side[:, bt, cols], in0=stack_bank[:], in1=bias_sum[:, cols], op=mybir.AluOpType.add
-            )
+                if i == 1:
+                    nc.vector.tensor_tensor(
+                        out=side[:, bt, cols], in0=banks[0][:], in1=bias_sum[:, cols], op=mybir.AluOpType.add
+                    )
+
+            return [lambda: multiply_stack(0), lambda: multiply_stack(1)]
 
         act_codes = keep.tile([P, PASSES, B], U32, align_bytes=64)
         act_scales = keep.tile([P, PASSES, B], U8, align_bytes=64)
 
-        def transpose_pass(raw, run_pitch, first_word, third_bank_on_vector):
+        def transpose_pass(raw, run_pitch, first_word, third_bank_on_vector, woven):
             raw_words = raw[:].bitcast(F32)
             grouped = grouped_pool.tile([P, 4 * ROWS], BF16, align_bytes=64)
             grouped_words = grouped[:].bitcast(F32).rearrange("p (r u) -> p r u", u=2)
@@ -169,6 +174,8 @@ def tile_stackrnn_pa_k_kernel(tc, x, hidden, stack_top, Wi, bi, Wh, bh, W0, b0, 
                         nc.tensor.transpose(
                             out=bank[:, a, u, :], in_=raw_words[:, word : word + P], identity=ident_f32[:]
                         )
+                    if a == 0 and woven:
+                        woven.pop(0)()
                 target = grouped_words[:, 2 * half * P : 2 * (half + 1) * P, :].rearrange("p (a r) u -> p a r u", a=2)
                 if third_bank_on_vector and half == 0:
                     nc.vector.tensor_copy(out=target, in_=bank[:].rearrange("p a u r -> p a r u"))
@@ -176,7 +183,7 @@ def tile_stackrnn_pa_k_kernel(tc, x, hidden, stack_top, Wi, bi, Wh, bh, W0, b0, 
                     nc.scalar.copy(out=target, in_=bank[:].rearrange("p a u r -> p a r u"))
             return grouped
 
-        def prepare(rnd, passes):
+        def prepare(rnd, passes, woven):
             wgt_codes = wgt_mx_pool.tile([P, len(passes), ROWS], U32, align_bytes=64)
             wgt_scales = wgt_mx_pool.tile([P, len(passes), ROWS], U8, align_bytes=64)
             jobs = []
@@ -185,7 +192,7 @@ def tile_stackrnn_pa_k_kernel(tc, x, hidden, stack_top, Wi, bi, Wh, bh, W0, b0, 
                 if rnd == 0:
                     jobs.append((act_raw[span][which], act_codes[:, c, :], act_scales[:, c, :]))
                 jobs.append((wgt_raw[(rnd, span)][which], wgt_codes[:, n, :], wgt_scales[:, n, :]))
-            grouped = [transpose_pass(*words, j % 2 == 1) for j, (words, codes, scales) in enumerate(jobs)]
+            grouped = [transpose_pass(*words, j % 2 == 1, woven) for j, (words, codes, scales) in enumerate(jobs)]
             for (words, codes, scales), values in zip(jobs, grouped):
                 nc.vector.quantize_mx(out=codes.bitcast(FP8X4), scales=scales, in_=values[:])
             return wgt_codes, wgt_scales
@@ -243,12 +250,10 @@ def tile_stackrnn_pa_k_kernel(tc, x, hidden, stack_top, Wi, bi, Wh, bh, W0, b0, 
         sums = {}
         waiting = None
         unstored = None
-        banks_of_side = [(rnd, bt) for rnd in range(ROUNDS) for bt in range(ROW_TILES)]
+        woven = [piece for rnd in range(ROUNDS) for bt in range(ROW_TILES) for piece in side_pieces(rnd, bt)]
         prepare_side()
         for step in steps + [None]:
-            for n in range(SIDE_BANKS.get(steps.index(step), 0) if step is not None else 0):
-                make_side(*banks_of_side.pop(0))
-            prepared = prepare(step[0], step[1]) if step is not None else None
+            prepared = prepare(step[0], step[1], woven) if step is not None else None
             if waiting is not None:
                 (rnd, passes), (wgt_codes, wgt_scales) = waiting
                 if passes[0] == 0:

@@ -159,8 +159,8 @@ def tile_stackrnn_pa_k_kernel(tc, x, hidden, stack_top, Wi, bi, Wh, bh, W0, b0, 
 
             return [lambda: multiply_stack(0), lambda: multiply_stack(1)]
 
-        act_codes = keep.tile([P, PASSES, B], U32, align_bytes=64)
-        act_scales = keep.tile([P, PASSES, B], U8, align_bytes=64)
+        act_codes = keep.tile([P, PASSES, B], U32, align_bytes=256)
+        act_scales = keep.tile([P, PASSES, B], U8, align_bytes=256)
 
         def transpose_pass(raw, run_pitch, first_word, third_bank_on_vector, woven):
             raw_words = raw[:].bitcast(F32)
@@ -184,8 +184,8 @@ def tile_stackrnn_pa_k_kernel(tc, x, hidden, stack_top, Wi, bi, Wh, bh, W0, b0, 
             return grouped
 
         def prepare(rnd, passes, woven):
-            wgt_codes = wgt_mx_pool.tile([P, len(passes), ROWS], U32, align_bytes=64)
-            wgt_scales = wgt_mx_pool.tile([P, len(passes), ROWS], U8, align_bytes=64)
+            wgt_codes = wgt_mx_pool.tile([P, len(passes), ROWS], U32, align_bytes=256)
+            wgt_scales = wgt_mx_pool.tile([P, len(passes), ROWS], U8, align_bytes=256)
             jobs = []
             for n, c in enumerate(passes):
                 span, which = divmod(c, PASSES_PER_SPAN)

from contextlib import ExitStack

import concourse.mybir as mybir
from concourse.masks import make_identity

F32 = mybir.dt.float32
BF16 = mybir.dt.bfloat16
U32 = mybir.dt.uint32
U8 = mybir.dt.uint8
FP8X4 = mybir.dt.float8_e4m3fn_x4

B, IDIM, HDIM, S = 512, 8192, 1024, 128
P = 128
K_PASS = 4 * P
K_SPAN = 2 * K_PASS
PASSES_PER_SPAN = K_SPAN // K_PASS
PASSES = (IDIM + HDIM) // K_PASS
ROWS = 512
ROW_TILES = ROWS // P
ROUNDS = HDIM // ROWS
WORDS_PER_PASS = K_PASS // 2
SPANS = PASSES // PASSES_PER_SPAN
TRANSPOSES_PER_PASS = 2 * ROW_TILES
TRANSPOSES_PER_BANK = 4
WARM_UP_MATMULS = 5
TRANSPOSES_PER_RUN = 16

FLOPS = 2 * B * HDIM * (IDIM + HDIM + 2 * S)


def tile_stackrnn_pa_k_kernel(tc, x, hidden, stack_top, Wi, bi, Wh, bh, W0, b0, W1, b1, out):
    nc = tc.nc
    with ExitStack() as ctx:
        keep = ctx.enter_context(tc.tile_pool(name="keep", bufs=1))
        act_raw_pool = ctx.enter_context(tc.tile_pool(name="act_raw", bufs=3))
        wgt_raw_pool = ctx.enter_context(tc.tile_pool(name="wgt_raw", bufs=4))
        grouped_pool = ctx.enter_context(tc.tile_pool(name="grouped", bufs=6))
        wgt_mx_pool = ctx.enter_context(tc.tile_pool(name="wgt_mx", bufs=2))
        result_pool = ctx.enter_context(tc.tile_pool(name="result", bufs=ROUNDS * ROW_TILES))
        work_psum = ctx.enter_context(tc.psum_pool(name="work_psum", bufs=4))
        sum_psum = ctx.enter_context(tc.psum_pool(name="sum_psum", bufs=1))
        ctx.enter_context(tc.manual_schedule())

        st_raw = keep.tile([P, 4, 2, S], BF16)
        st_raw = keep.tile([P, 4, 2, S], BF16)
        w01_raw = keep.tile([P, 2, 8, S], BF16)

        def load_small():
            nc.sync.dma_start(out=st_raw[:], in_=stack_top.rearrange("(p t) i s -> p t i s", t=4))
            nc.sync.dma_start(out=w01_raw[:, 0], in_=W0.rearrange("(p t) s -> p t s", t=8))
            nc.sync.dma_start(out=w01_raw[:, 1], in_=W1.rearrange("(p t) s -> p t s", t=8))

        def load_span(pool, span, from_x, from_hidden, first_row, passes_per_load):
            k = span * K_SPAN
            source, k = (from_x, k) if k < IDIM else (from_hidden, k - IDIM)
            raw = pool.tile([P, ROW_TILES * K_SPAN], BF16, name="raw")
            width = passes_per_load * K_PASS
            words = []
            loads = []
            for first in range(0, PASSES_PER_SPAN, passes_per_load):
                start = first * ROW_TILES * K_PASS
                loads.append(
                    (
                        raw[:, start : start + ROW_TILES * width].rearrange("p (t k) -> p t k", t=ROW_TILES),
                        source[
                            first_row : first_row + ROWS, k + first * K_PASS : k + first * K_PASS + width
                        ].rearrange("(t p) k -> p t k", p=P),
                    )
                )
                words += [(raw, width // 2, start // 2 + n * WORDS_PER_PASS) for n in range(passes_per_load)]
            return words, loads

        act_raw = {}
        wgt_raw = {}
        load_small()
        for rnd in range(ROUNDS):
            for span in range(SPANS):
                passes_per_load = 1 if (rnd, span) == (0, 0) else PASSES_PER_SPAN
                loads = []
                if rnd == 0:
                    act_raw[span], act_loads = load_span(act_raw_pool, span, x, hidden, 0, passes_per_load)
                    loads.append(act_loads)
                wgt_raw[(rnd, span)], wgt_loads = load_span(wgt_raw_pool, span, Wi, Wh, rnd * ROWS, passes_per_load)
                loads.append(wgt_loads)
                for together in zip(*loads):
                    for target, source in together:
                        nc.sync.dma_start(out=target, in_=source)

        zeros = keep.tile([P, ROWS], BF16)
        nc.gpsimd.memset(zeros[:].bitcast(F32), 0.0)
        warm_bank = work_psum.tile([P, ROWS], F32, tag="work")

        def warm_up(matmuls):
            for n in range(matmuls):
                nc.tensor.matmul(out=warm_bank[:], lhsT=zeros[:, :P], rhs=zeros[:], start=True, stop=True)

        warm_up(WARM_UP_MATMULS)

        bias_rows = keep.tile([P, HDIM], BF16)
        nc.vector.memset(bias_rows[:].bitcast(F32), 0.0)
        for row, bias in enumerate((bi, bh, b0, b1)):
            nc.scalar.dma_start(out=bias_rows[row : row + 1, :], in_=bias.rearrange("(o n) -> o n", o=1))
        ones = keep.tile([P, P], BF16)
        nc.vector.memset(ones[:], 1.0)

        ident_bf16 = keep.tile([P, P], BF16)
        make_identity(nc, ident_bf16[:])
        ident_f32 = keep.tile([P, P], F32)
        make_identity(nc, ident_f32[:])

        warm = keep.tile([P, 1], F32)
        nc.vector.memset(warm[:], 0.0)
        nc.scalar.activation(out=warm[:], in_=warm[:], func=mybir.ActivationFunctionType.Sigmoid)

        st_T = keep.tile([P, 2, B], BF16)
        w01_T = keep.tile([P, 2, HDIM], BF16)
        bias_sum = keep.tile([P, HDIM], F32)

        def prepare_side():
            st_bank = work_psum.tile([P, 4, 2, P], BF16, tag="work")
            for t in range(4):
                for i in range(2):
                    nc.tensor.transpose(out=st_bank[:, t, i, :], in_=st_raw[:, t, i, :], identity=ident_bf16[:])
            nc.vector.tensor_copy(
                out=st_T[:].rearrange("s i (p t) -> s i p t", t=4), in_=st_bank[:].rearrange("s t i p -> s i p t")
            )
            warm_up(2)
            for i in range(2):
                w_bank = work_psum.tile([P, 8, P], BF16, tag="work")
                for t in range(8):
                    nc.tensor.transpose(out=w_bank[:, t, :], in_=w01_raw[:, i, t, :], identity=ident_bf16[:])
                copy_out = nc.scalar.copy if i == 0 else nc.vector.tensor_copy
                copy_out(out=w01_T[:, i, :].rearrange("s (p t) -> s p t", t=8), in_=w_bank[:].rearrange("s t p -> s p t"))

            for rnd in range(ROUNDS):
                cols = slice(rnd * ROWS, (rnd + 1) * ROWS)
                bias_bank = work_psum.tile([P, ROWS], F32, tag="work")
                nc.tensor.matmul(out=bias_bank[:], lhsT=ones[:], rhs=bias_rows[:, cols], start=True, stop=True)
                nc.scalar.copy(out=bias_sum[:, cols], in_=bias_bank[:])


        side = keep.tile([P, ROW_TILES, HDIM], F32)

        def side_pieces(rnd, bt):
            cols = slice(rnd * ROWS, (rnd + 1) * ROWS)
            rows = slice(bt * P, (bt + 1) * P)
            banks = []

            def multiply_stack(i):
                if i == 0:
                    banks.append(work_psum.tile([P, ROWS], F32, tag="work", name="stack_bank"))
                nc.tensor.matmul(
                    out=banks[0][:], lhsT=st_T[:, i, rows], rhs=w01_T[:, i, cols], start=(i == 0), stop=(i == 1)
                )
                if i == 1:
                    nc.vector.tensor_tensor(
                        out=side[:, bt, cols], in0=banks[0][:], in1=bias_sum[:, cols], op=mybir.AluOpType.add
                    )

            return [lambda: multiply_stack(0), lambda: multiply_stack(1)]

        act_codes = keep.tile([P, PASSES, B], U32, align_bytes=256)
        act_scales = keep.tile([P, PASSES, B], U8, align_bytes=256)

        def transpose_pass(raw, run_pitch, first_word, third_bank_on_vector, woven):
            raw_words = raw[:].bitcast(F32)
            grouped = grouped_pool.tile([P, 4 * ROWS], BF16, align_bytes=64)
            grouped_words = grouped[:].bitcast(F32).rearrange("p (r u) -> p r u", u=2)
            for half in range(TRANSPOSES_PER_PASS // TRANSPOSES_PER_BANK):
                bank = work_psum.tile([P, 2, 2, P], F32, tag="work")
                for a in range(2):
                    for u in range(2):
                        word = (2 * half + a) * run_pitch + first_word + u * P
                        nc.tensor.transpose(
                            out=bank[:, a, u, :], in_=raw_words[:, word : word + P], identity=ident_f32[:]
                        )
                    if a == 0 and woven:
                        woven.pop(0)()
                target = grouped_words[:, 2 * half * P : 2 * (half + 1) * P, :].rearrange("p (a r) u -> p a r u", a=2)
                if third_bank_on_vector and half == 0:
                    nc.vector.tensor_copy(out=target, in_=bank[:].rearrange("p a u r -> p a r u"))
                else:
                    nc.scalar.copy(out=target, in_=bank[:].rearrange("p a u r -> p a r u"))
            return grouped

        def prepare(rnd, passes, woven):
            wgt_codes = wgt_mx_pool.tile([P, len(passes), ROWS], U32, align_bytes=256)
            wgt_scales = wgt_mx_pool.tile([P, len(passes), ROWS], U8, align_bytes=256)
            jobs = []
            for n, c in enumerate(passes):
                span, which = divmod(c, PASSES_PER_SPAN)
                if rnd == 0:
                    jobs.append((act_raw[span][which], act_codes[:, c, :], act_scales[:, c, :]))
                jobs.append((wgt_raw[(rnd, span)][which], wgt_codes[:, n, :], wgt_scales[:, n, :]))
            grouped = [transpose_pass(*words, j % 2 == 1, woven) for j, (words, codes, scales) in enumerate(jobs)]
            for (words, codes, scales), values in zip(jobs, grouped):
                nc.vector.quantize_mx(out=codes.bitcast(FP8X4), scales=scales, in_=values[:])
            return wgt_codes, wgt_scales

        def multiply(sums, passes, wgt_codes, wgt_scales):
            for bt in range(ROW_TILES):
                rows = slice(bt * P, (bt + 1) * P)
                for n, c in enumerate(passes):
                    nc.tensor.matmul_mx(
                        out=sums[bt][:],
                        lhsT=act_codes[:, c, rows].bitcast(FP8X4),
                        lhsT_scale=act_scales[:, c, rows],
                        rhs=wgt_codes[:, n, :].bitcast(FP8X4),
                        rhs_scale=wgt_scales[:, n, :],
                        start=(c == 0),
                        stop=(c == PASSES - 1),
                    )

        def pieces_of(rnd, bt):
            n = 2 if rnd == ROUNDS - 1 and bt == ROW_TILES - 1 else 1
            return [slice(i * ROWS // n, (i + 1) * ROWS // n) for i in range(n)]

        def add_side(rnd, sums):
            results = []
            for bt in range(ROW_TILES):
                result = result_pool.tile([P, ROWS], F32, name="result")
                for cols in pieces_of(rnd, bt):
                    nc.vector.tensor_tensor(
                        out=result[:, cols],
                        in0=sums[bt][:, cols],
                        in1=side[:, bt, rnd * ROWS + cols.start : rnd * ROWS + cols.stop],
                        op=mybir.AluOpType.add,
                    )
                results.append(result)
            return results

        def store(rnd, results):
            for bt, result in enumerate(results):
                for cols in pieces_of(rnd, bt):
                    nc.scalar.activation(
                        out=result[:, cols], in_=result[:, cols], func=mybir.ActivationFunctionType.Sigmoid
                    )
                    nc.sync.dma_start(
                        out=out[bt * P : (bt + 1) * P, rnd * ROWS + cols.start : rnd * ROWS + cols.stop],
                        in_=result[:, cols],
                    )

        steps = []
        for rnd in range(ROUNDS):
            operands_to_make = 2 if rnd == 0 else 1
            passes_per_step = TRANSPOSES_PER_RUN // (operands_to_make * TRANSPOSES_PER_PASS)
            for first in range(0, PASSES, passes_per_step):
                steps.append((rnd, list(range(first, min(first + passes_per_step, PASSES)))))

        sums = {}
        waiting = None
        unstored = None
        woven = [piece for rnd in range(ROUNDS) for bt in range(ROW_TILES) for piece in side_pieces(rnd, bt)]
        prepare_side()
        for step in steps + [None]:
            prepared = prepare(step[0], step[1], woven) if step is not None else None
            if waiting is not None:
                (rnd, passes), (wgt_codes, wgt_scales) = waiting
                if passes[0] == 0:
                    sums[rnd] = [sum_psum.tile([P, ROWS], F32, name="sum%d" % bt) for bt in range(ROW_TILES)]
                multiply(sums[rnd], passes, wgt_codes, wgt_scales)
                if unstored is not None:
                    store(*unstored)
                    unstored = None
                if passes[-1] == PASSES - 1:
                    unstored = (rnd, add_side(rnd, sums[rnd]))
            waiting = (step, prepared)
        store(*unstored)
